import numpy as np
import ml_dtypes


def mxq(x, axis, fmt="e4m3"):
    dtype, down = {"e4m3": (ml_dtypes.float8_e4m3fn, 7), "e5m2": (ml_dtypes.float8_e5m2, 14)}[fmt]
    v = np.moveaxis(np.asarray(x, np.float32).astype(ml_dtypes.bfloat16).astype(np.float64), axis, -1)
    blocks = v.reshape(v.shape[:-1] + (-1, 32))
    amax = np.abs(blocks).max(-1, keepdims=True)
    byte = np.maximum(np.where(amax > 0, np.frexp(amax)[1] - 1 + 127, 0) - down, 1)
    scale = np.exp2(byte - 127.0)
    codes = (blocks / scale).astype(np.float32).astype(dtype).astype(np.float64)
    return np.moveaxis((codes * scale).reshape(v.shape), -1, axis)


WIDE = False


def mx_kscale(k):
    if not WIDE:
        return np.ones(k)
    levels = np.array([20, -20, 10, -10, 0])
    a = np.random.permutation(np.resize(levels, k // 512 * 4)).reshape(k // 512, 4)
    idx = np.arange(k)
    return np.exp2(a[idx // 512, idx % 128 // 32])


BF16 = ml_dtypes.bfloat16


def bf(x):
    return np.asarray(x, np.float32).astype(BF16)


def f64(x):
    return np.asarray(x).astype(np.float64)


N, I, O = 8192, 512, 512


def setup_inputs():
    u = mx_kscale(O)
    mask = np.tile(np.array([0.0, 0.0, 1.0, 1.0]), I // 4)
    gd = mask + 0.1 * (1.0 - mask)
    gs = (1.0 - mask) + 0.1 * mask
    x = np.random.standard_normal((N, I))
    wd = np.random.standard_normal((O, I)) * gd / np.sqrt(I) / u[:, None]
    ws = np.random.standard_normal((O, I)) * gs / np.sqrt(I) / u[:, None]
    g = np.random.standard_normal((N, O)) * np.exp2(np.random.randint(-12, 1, (N, 1))) * 8.0 * u
    return {"x": bf(x), "W_dense": bf(wd), "W_sparse": bf(ws), "grad_out": bf(g)}


def reference(x, W_dense, W_sparse, grad_out):
    gq = mxq(f64(grad_out), 1, "e5m2")
    gx_dense = gq @ mxq(f64(W_dense), 0, "e4m3")
    gx_sparse = gq @ mxq(f64(W_sparse), 0, "e4m3")
    return gx_dense + gx_sparse

@@ -1,0 +1,153 @@
+from contextlib import ExitStack
+
+import concourse.mybir as mybir
+from concourse.masks import make_identity
+
+BF16 = mybir.dt.bfloat16
+F32 = mybir.dt.float32
+U32 = mybir.dt.uint32
+U8 = mybir.dt.uint8
+E4M3_X4 = mybir.dt.float8_e4m3fn_x4
+E5M2_X4 = mybir.dt.float8_e5m2_x4
+
+P = 128
+PACK = 4
+TOKENS = 8192
+K = 512
+COLS = 512
+PAIRS = K // 2
+
+TOKEN_TILES = TOKENS // P
+ROUND_TILES = 8
+HALF_TILES = ROUND_TILES // 2
+ROUNDS = TOKEN_TILES // ROUND_TILES
+BANK_TILES = 2
+ROUND_BANKS = ROUND_TILES // BANK_TILES
+HALF_BANKS = ROUND_BANKS // 2
+
+FLOPS = 2 * 2 * TOKENS * K * COLS
+BYTES = TOKENS * K * 2 + 2 * K * COLS * 2 + TOKENS * COLS * 4
+
+
+def tile_myinterleavedmodule_t_kernel(tc, x, W_dense, W_sparse, grad_out, out):
+    nc = tc.nc
+
+    grad_rows = grad_out.rearrange("(p j) k -> p (j k)", j=TOKEN_TILES)
+    out_rows = out.rearrange("(p j) c -> p (j c)", j=TOKEN_TILES)
+
+    with ExitStack() as ctx:
+        ctx.enter_context(tc.manual_schedule())
+        keep = ctx.enter_context(tc.tile_pool(name="keep", bufs=1))
+        work = ctx.enter_context(tc.tile_pool(name="work", bufs=2))
+        results = ctx.enter_context(tc.tile_pool(name="results", bufs=4))
+        flipped_banks = ctx.enter_context(tc.psum_pool(name="flipped_banks", bufs=ROUND_BANKS))
+        sum_banks = ctx.enter_context(tc.psum_pool(name="sum_banks", bufs=4))
+
+        weight_raw = {}
+        for name, weight in (("dense", W_dense), ("sparse", W_sparse)):
+            raw = keep.tile([P, PACK, COLS], BF16, name="raw_" + name)
+            nc.sync.dma_start(
+                out=raw[:].rearrange("q (u e) c -> q u (e c)", u=2),
+                in_=weight.rearrange("(u q e) c -> q u (e c)", u=2, e=2),
+            )
+            weight_raw[name] = raw
+        grad_raw = []
+        for r in range(ROUNDS):
+            raw = keep.tile([P, ROUND_TILES * K], BF16, name="grad_raw%d" % r)
+            pieces = 2 if r == 0 else 1
+            width = ROUND_TILES * K // pieces
+            for piece in range(pieces):
+                first = r * ROUND_TILES * K + piece * width
+                nc.sync.dma_start(
+                    out=raw[:, piece * width : (piece + 1) * width],
+                    in_=grad_rows[:, first : first + width],
+                )
+            grad_raw.append(raw)
+
+        identity = keep.tile([P, P], F32, name="identity")
+        make_identity(nc, identity[:])
+
+        weight_codes = {}
+        weight_scales = {}
+        for name in ("dense", "sparse"):
+            grouped = keep.tile([P, COLS, PACK], BF16, name="grouped_" + name, align_bytes=64)
+            nc.vector.tensor_copy(
+                out=grouped[:], in_=weight_raw[name][:].rearrange("q t c -> q c t")
+            )
+            codes = keep.tile([P, COLS], U32, name="codes_" + name, align_bytes=64)
+            scales = keep.tile([P, COLS], U8, name="scales_" + name, align_bytes=64)
+            nc.vector.quantize_mx(
+                out=codes[:].bitcast(E4M3_X4),
+                scales=scales[:],
+                in_=grouped[:].rearrange("q c t -> q (c t)"),
+            )
+            weight_codes[name] = codes
+            weight_scales[name] = scales
+
+        def transpose_and_quantise(r):
+            pairs = grad_raw[r][:].bitcast(F32)
+            grouped = work.tile([P, ROUND_TILES * K], BF16, name="grouped", align_bytes=64)
+            grouped_pairs = grouped[:].bitcast(F32)
+            codes = work.tile([P, ROUND_TILES * P], U32, name="codes", align_bytes=64)
+            scales = work.tile([P, ROUND_TILES * P], U8, name="scales", align_bytes=64)
+            copy_out = nc.scalar.copy if r == 0 else nc.vector.tensor_copy
+            for b in range(ROUND_BANKS):
+                flipped = flipped_banks.tile([P, BANK_TILES * PAIRS], F32, name="flipped")
+                for block in range(BANK_TILES * 2):
+                    first = (b * BANK_TILES * 2 + block) * P
+                    nc.tensor.transpose(
+                        flipped[:, block * P : (block + 1) * P],
+                        pairs[:, first : first + P],
+                        identity[:],
+                    )
+                copy_out(
+                    out=grouped_pairs[
+                        :, b * BANK_TILES * PAIRS : (b + 1) * BANK_TILES * PAIRS
+                    ].rearrange("q (j m u) -> q j m u", j=BANK_TILES, u=2),
+                    in_=flipped[:].rearrange("q (j u m) -> q j m u", j=BANK_TILES, u=2),
+                )
+                if (b + 1) % HALF_BANKS == 0:
+                    half = b // HALF_BANKS
+                    words = slice(half * HALF_TILES * P, (half + 1) * HALF_TILES * P)
+                    nc.vector.quantize_mx(
+                        out=codes[:, words].bitcast(E5M2_X4),
+                        scales=scales[:, words],
+                        in_=grouped[:, half * HALF_TILES * K : (half + 1) * HALF_TILES * K],
+                    )
+            return codes, scales
+
+        def store(r, result, first, count):
+            nc.sync.dma_start(
+                out=out_rows[:, (r * ROUND_TILES + first) * COLS : (r * ROUND_TILES + first + count) * COLS],
+                in_=result[:, first * COLS : (first + count) * COLS],
+            )
+
+        def multiply(r, half, codes, scales, result):
+            last_half = r == ROUNDS - 1 and half == 1
+            for j in range(half * HALF_TILES, (half + 1) * HALF_TILES):
+                tokens = slice(j * P, (j + 1) * P)
+                sums = sum_banks.tile([P, COLS], F32, name="sums")
+                for name in ("dense", "sparse"):
+                    nc.tensor.matmul_mx(
+                        out=sums[:],
+                        lhsT=codes[:, tokens].bitcast(E5M2_X4),
+                        lhsT_scale=scales[:, tokens],
+                        rhs=weight_codes[name][:].bitcast(E4M3_X4),
+                        rhs_scale=weight_scales[name][:],
+                        start=(name == "dense"),
+                        stop=(name == "sparse"),
+                    )
+                nc.scalar.copy(out=result[:, j * COLS : (j + 1) * COLS], in_=sums[:])
+                if last_half:
+                    store(r, result, j, 1)
+            if not last_half:
+                store(r, result, half * HALF_TILES, HALF_TILES)
+
+        quantised = transpose_and_quantise(0)
+        for r in range(ROUNDS):
+            codes, scales = quantised
+            result = results.tile([P, ROUND_TILES * COLS], F32, name="result")
+            multiply(r, 0, codes, scales, result)
+            if r + 1 < ROUNDS:
+                quantised = transpose_and_quantise(r + 1)
+            multiply(r, 1, codes, scales, result)

@@ -32,8 +32,8 @@ BYTES = TOKENS * K * 2 + 2 * K * COLS * 2 + TOKENS * COLS * 4
 def tile_myinterleavedmodule_t_kernel(tc, x, W_dense, W_sparse, grad_out, out):
     nc = tc.nc
 
-    grad_rows = grad_out.rearrange("(p j) k -> p (j k)", j=TOKEN_TILES)
-    out_rows = out.rearrange("(p j) c -> p (j c)", j=TOKEN_TILES)
+    grad_rows = grad_out.rearrange("(r p j) k -> r p (j k)", p=P, j=ROUND_TILES)
+    out_rows = out.rearrange("(r p j) c -> r p (j c)", p=P, j=ROUND_TILES)
 
     with ExitStack() as ctx:
         ctx.enter_context(tc.manual_schedule())
@@ -57,10 +57,9 @@ def tile_myinterleavedmodule_t_kernel(tc, x, W_dense, W_sparse, grad_out, out):
             pieces = 2 if r == 0 else 1
             width = ROUND_TILES * K // pieces
             for piece in range(pieces):
-                first = r * ROUND_TILES * K + piece * width
                 nc.sync.dma_start(
                     out=raw[:, piece * width : (piece + 1) * width],
-                    in_=grad_rows[:, first : first + width],
+                    in_=grad_rows[r, :, piece * width : (piece + 1) * width],
                 )
             grad_raw.append(raw)
 
@@ -118,7 +117,7 @@ def tile_myinterleavedmodule_t_kernel(tc, x, W_dense, W_sparse, grad_out, out):
 
         def store(r, result, first, count):
             nc.sync.dma_start(
-                out=out_rows[:, (r * ROUND_TILES + first) * COLS : (r * ROUND_TILES + first + count) * COLS],
+                out=out_rows[r, :, first * COLS : (first + count) * COLS],
                 in_=result[:, first * COLS : (first + count) * COLS],
             )
 

@@ -20,6 +20,7 @@ PAIRS = K // 2
 TOKEN_TILES = TOKENS // P
 ROUND_TILES = 8
 HALF_TILES = ROUND_TILES // 2
+TILES_BEFORE_RUN = 2
 ROUNDS = TOKEN_TILES // ROUND_TILES
 BANK_TILES = 2
 ROUND_BANKS = ROUND_TILES // BANK_TILES
@@ -121,9 +122,8 @@ def tile_myinterleavedmodule_t_kernel(tc, x, W_dense, W_sparse, grad_out, out):
                 in_=result[:, first * COLS : (first + count) * COLS],
             )
 
-        def multiply(r, half, codes, scales, result):
-            last_half = r == ROUNDS - 1 and half == 1
-            for j in range(half * HALF_TILES, (half + 1) * HALF_TILES):
+        def multiply(r, tiles, codes, scales, result):
+            for j in tiles:
                 tokens = slice(j * P, (j + 1) * P)
                 sums = sum_banks.tile([P, COLS], F32, name="sums")
                 for name in ("dense", "sparse"):
@@ -137,16 +137,16 @@ def tile_myinterleavedmodule_t_kernel(tc, x, W_dense, W_sparse, grad_out, out):
                         stop=(name == "sparse"),
                     )
                 nc.scalar.copy(out=result[:, j * COLS : (j + 1) * COLS], in_=sums[:])
-                if last_half:
+                if r == ROUNDS - 1 and j >= HALF_TILES:
                     store(r, result, j, 1)
-            if not last_half:
-                store(r, result, half * HALF_TILES, HALF_TILES)
+                elif (j + 1) % HALF_TILES == 0:
+                    store(r, result, j + 1 - HALF_TILES, HALF_TILES)
 
         quantised = transpose_and_quantise(0)
         for r in range(ROUNDS):
             codes, scales = quantised
             result = results.tile([P, ROUND_TILES * COLS], F32, name="result")
-            multiply(r, 0, codes, scales, result)
+            multiply(r, range(TILES_BEFORE_RUN), codes, scales, result)
             if r + 1 < ROUNDS:
                 quantised = transpose_and_quantise(r + 1)
-            multiply(r, 1, codes, scales, result)
+            multiply(r, range(TILES_BEFORE_RUN, ROUND_TILES), codes, scales, result)

@@ -20,11 +20,12 @@ PAIRS = K // 2
 TOKEN_TILES = TOKENS // P
 ROUND_TILES = 8
 HALF_TILES = ROUND_TILES // 2
-TILES_BEFORE_RUN = 2
 ROUNDS = TOKEN_TILES // ROUND_TILES
 BANK_TILES = 2
 ROUND_BANKS = ROUND_TILES // BANK_TILES
-HALF_BANKS = ROUND_BANKS // 2
+TILES_BEFORE_RUN = 2
+TILES_BEFORE_FIRST_RUN = 6
+VECTOR_COLS = 352
 
 FLOPS = 2 * 2 * TOKENS * K * COLS
 BYTES = TOKENS * K * 2 + 2 * K * COLS * 2 + TOKENS * COLS * 4
@@ -45,35 +46,43 @@ def tile_myinterleavedmodule_t_kernel(tc, x, W_dense, W_sparse, grad_out, out):
         sum_banks = ctx.enter_context(tc.psum_pool(name="sum_banks", bufs=4))
 
         weight_raw = {}
-        for name, weight in (("dense", W_dense), ("sparse", W_sparse)):
+        grad_raw = [
+            keep.tile([P, ROUND_TILES * K], BF16, name="grad_raw%d" % r) for r in range(ROUNDS)
+        ]
+
+        def load_weight(name, weight):
             raw = keep.tile([P, PACK, COLS], BF16, name="raw_" + name)
             nc.sync.dma_start(
                 out=raw[:].rearrange("q (u e) c -> q u (e c)", u=2),
                 in_=weight.rearrange("(u q e) c -> q u (e c)", u=2, e=2),
             )
             weight_raw[name] = raw
-        grad_raw = []
-        for r in range(ROUNDS):
-            raw = keep.tile([P, ROUND_TILES * K], BF16, name="grad_raw%d" % r)
-            pieces = 2 if r == 0 else 1
-            width = ROUND_TILES * K // pieces
-            for piece in range(pieces):
-                nc.sync.dma_start(
-                    out=raw[:, piece * width : (piece + 1) * width],
-                    in_=grad_rows[r, :, piece * width : (piece + 1) * width],
-                )
-            grad_raw.append(raw)
+
+        def load_grad(r, first, count):
+            nc.sync.dma_start(
+                out=grad_raw[r][:, first * K : (first + count) * K],
+                in_=grad_rows[r, :, first * K : (first + count) * K],
+            )
+
+        load_weight("dense", W_dense)
+        load_grad(0, 0, BANK_TILES)
+        load_grad(0, BANK_TILES, BANK_TILES)
+        load_weight("sparse", W_sparse)
+        load_grad(0, HALF_TILES, HALF_TILES)
+        for r in range(1, ROUNDS):
+            load_grad(r, 0, ROUND_TILES)
 
         identity = keep.tile([P, P], F32, name="identity")
         make_identity(nc, identity[:])
 
         weight_codes = {}
         weight_scales = {}
-        for name in ("dense", "sparse"):
+
+        def quantise_weight(name):
             grouped = keep.tile([P, COLS, PACK], BF16, name="grouped_" + name, align_bytes=64)
-            nc.vector.tensor_copy(
-                out=grouped[:], in_=weight_raw[name][:].rearrange("q t c -> q c t")
-            )
+            by_column = weight_raw[name][:].rearrange("q t c -> q c t")
+            nc.vector.tensor_copy(out=grouped[:, :VECTOR_COLS, :], in_=by_column[:, :VECTOR_COLS, :])
+            nc.scalar.copy(out=grouped[:, VECTOR_COLS:, :], in_=by_column[:, VECTOR_COLS:, :])
             codes = keep.tile([P, COLS], U32, name="codes_" + name, align_bytes=64)
             scales = keep.tile([P, COLS], U8, name="scales_" + name, align_bytes=64)
             nc.vector.quantize_mx(
@@ -84,37 +93,56 @@ def tile_myinterleavedmodule_t_kernel(tc, x, W_dense, W_sparse, grad_out, out):
             weight_codes[name] = codes
             weight_scales[name] = scales
 
-        def transpose_and_quantise(r):
-            pairs = grad_raw[r][:].bitcast(F32)
+        def new_round():
             grouped = work.tile([P, ROUND_TILES * K], BF16, name="grouped", align_bytes=64)
-            grouped_pairs = grouped[:].bitcast(F32)
             codes = work.tile([P, ROUND_TILES * P], U32, name="codes", align_bytes=64)
             scales = work.tile([P, ROUND_TILES * P], U8, name="scales", align_bytes=64)
-            copy_out = nc.scalar.copy if r == 0 else nc.vector.tensor_copy
-            for b in range(ROUND_BANKS):
-                flipped = flipped_banks.tile([P, BANK_TILES * PAIRS], F32, name="flipped")
-                for block in range(BANK_TILES * 2):
-                    first = (b * BANK_TILES * 2 + block) * P
-                    nc.tensor.transpose(
-                        flipped[:, block * P : (block + 1) * P],
-                        pairs[:, first : first + P],
-                        identity[:],
-                    )
-                copy_out(
-                    out=grouped_pairs[
-                        :, b * BANK_TILES * PAIRS : (b + 1) * BANK_TILES * PAIRS
-                    ].rearrange("q (j m u) -> q j m u", j=BANK_TILES, u=2),
-                    in_=flipped[:].rearrange("q (j u m) -> q j m u", j=BANK_TILES, u=2),
+            return grouped, codes, scales
+
+        def transpose_bank(r, b, grouped, copy_out):
+            pairs = grad_raw[r][:].bitcast(F32)
+            flipped = flipped_banks.tile([P, BANK_TILES * PAIRS], F32, name="flipped")
+            for block in range(BANK_TILES * 2):
+                first = (b * BANK_TILES * 2 + block) * P
+                nc.tensor.transpose(
+                    flipped[:, block * P : (block + 1) * P],
+                    pairs[:, first : first + P],
+                    identity[:],
                 )
-                if (b + 1) % HALF_BANKS == 0:
-                    half = b // HALF_BANKS
-                    words = slice(half * HALF_TILES * P, (half + 1) * HALF_TILES * P)
-                    nc.vector.quantize_mx(
-                        out=codes[:, words].bitcast(E5M2_X4),
-                        scales=scales[:, words],
-                        in_=grouped[:, half * HALF_TILES * K : (half + 1) * HALF_TILES * K],
-                    )
+            copy_out(
+                out=grouped[:]
+                .bitcast(F32)[:, b * BANK_TILES * PAIRS : (b + 1) * BANK_TILES * PAIRS]
+                .rearrange("q (j m u) -> q j m u", j=BANK_TILES, u=2),
+                in_=flipped[:].rearrange("q (j u m) -> q j m u", j=BANK_TILES, u=2),
+            )
+
+        def quantise_tiles(first, count, grouped, codes, scales):
+            words = slice(first * P, (first + count) * P)
+            nc.vector.quantize_mx(
+                out=codes[:, words].bitcast(E5M2_X4),
+                scales=scales[:, words],
+                in_=grouped[:, first * K : (first + count) * K],
+            )
+
+        def transpose_and_quantise(r):
+            grouped, codes, scales = new_round()
+            for b in range(ROUND_BANKS):
+                transpose_bank(r, b, grouped, nc.vector.tensor_copy)
+                if (b + 1) * BANK_TILES % HALF_TILES == 0:
+                    quantise_tiles((b + 1) * BANK_TILES - HALF_TILES, HALF_TILES, grouped, codes, scales)
             return codes, scales
+
+        def product(name, j, codes, scales, sums):
+            tokens = slice(j * P, (j + 1) * P)
+            nc.tensor.matmul_mx(
+                out=sums[:],
+                lhsT=codes[:, tokens].bitcast(E5M2_X4),
+                lhsT_scale=scales[:, tokens],
+                rhs=weight_codes[name][:].bitcast(E4M3_X4),
+                rhs_scale=weight_scales[name][:],
+                start=(name == "dense"),
+                stop=(name == "sparse"),
+            )
 
         def store(r, result, first, count):
             nc.sync.dma_start(
@@ -122,28 +150,44 @@ def tile_myinterleavedmodule_t_kernel(tc, x, W_dense, W_sparse, grad_out, out):
                 in_=result[:, first * COLS : (first + count) * COLS],
             )
 
+        def leave(r, j, sums, result):
+            nc.scalar.copy(out=result[:, j * COLS : (j + 1) * COLS], in_=sums[:])
+            if r == ROUNDS - 1 and j >= HALF_TILES:
+                store(r, result, j, 1)
+            elif (j + 1) % HALF_TILES == 0:
+                store(r, result, j + 1 - HALF_TILES, HALF_TILES)
+
         def multiply(r, tiles, codes, scales, result):
             for j in tiles:
-                tokens = slice(j * P, (j + 1) * P)
                 sums = sum_banks.tile([P, COLS], F32, name="sums")
-                for name in ("dense", "sparse"):
-                    nc.tensor.matmul_mx(
-                        out=sums[:],
-                        lhsT=codes[:, tokens].bitcast(E5M2_X4),
-                        lhsT_scale=scales[:, tokens],
-                        rhs=weight_codes[name][:].bitcast(E4M3_X4),
-                        rhs_scale=weight_scales[name][:],
-                        start=(name == "dense"),
-                        stop=(name == "sparse"),
-                    )
-                nc.scalar.copy(out=result[:, j * COLS : (j + 1) * COLS], in_=sums[:])
-                if r == ROUNDS - 1 and j >= HALF_TILES:
-                    store(r, result, j, 1)
-                elif (j + 1) % HALF_TILES == 0:
-                    store(r, result, j + 1 - HALF_TILES, HALF_TILES)
+                product("dense", j, codes, scales, sums)
+                product("sparse", j, codes, scales, sums)
+                leave(r, j, sums, result)
 
-        quantised = transpose_and_quantise(0)
-        for r in range(ROUNDS):
+        grouped, codes, scales = new_round()
+        result = results.tile([P, ROUND_TILES * COLS], F32, name="result")
+        quantise_weight("dense")
+        for b in range(HALF_TILES // BANK_TILES):
+            transpose_bank(0, b, grouped, nc.scalar.copy)
+            quantise_tiles(b * BANK_TILES, BANK_TILES, grouped, codes, scales)
+        quantise_weight("sparse")
+        open_sums = []
+        for j in range(HALF_TILES):
+            sums = sum_banks.tile([P, COLS], F32, name="sums")
+            product("dense", j, codes, scales, sums)
+            open_sums.append(sums)
+        transpose_bank(0, 2, grouped, nc.scalar.copy)
+        transpose_bank(0, 3, grouped, nc.vector.tensor_copy)
+        quantise_tiles(2 * BANK_TILES, BANK_TILES, grouped, codes, scales)
+        quantise_tiles(3 * BANK_TILES, BANK_TILES, grouped, codes, scales)
+        for j in range(HALF_TILES):
+            product("sparse", j, codes, scales, open_sums[j])
+            leave(0, j, open_sums[j], result)
+        multiply(0, range(HALF_TILES, TILES_BEFORE_FIRST_RUN), codes, scales, result)
+        quantised = transpose_and_quantise(1)
+        multiply(0, range(TILES_BEFORE_FIRST_RUN, ROUND_TILES), codes, scales, result)
+
+        for r in range(1, ROUNDS):
             codes, scales = quantised
             result = results.tile([P, ROUND_TILES * COLS], F32, name="result")
             multiply(r, range(TILES_BEFORE_RUN), codes, scales, result)

@@ -25,6 +25,8 @@ BANK_TILES = 2
 ROUND_BANKS = ROUND_TILES // BANK_TILES
 TILES_BEFORE_RUN = 2
 TILES_BEFORE_FIRST_RUN = 6
+WARM_UP_PASSES = 7
+GAP_PASSES = 2
 VECTOR_COLS = 352
 
 FLOPS = 2 * 2 * TOKENS * K * COLS
@@ -74,6 +76,16 @@ def tile_myinterleavedmodule_t_kernel(tc, x, W_dense, W_sparse, grad_out, out):
 
         identity = keep.tile([P, P], F32, name="identity")
         make_identity(nc, identity[:])
+
+        zeros = keep.tile([P, COLS], BF16, name="zeros")
+        nc.vector.memset(zeros[:], 0.0)
+        unread = sum_banks.tile([P, COLS], F32, name="sums")
+
+        def idle_passes(count):
+            for i in range(count):
+                nc.tensor.matmul(unread[:], lhsT=zeros[:, :P], rhs=zeros[:], start=True, stop=True)
+
+        idle_passes(WARM_UP_PASSES)
 
         weight_codes = {}
         weight_scales = {}
@@ -171,6 +183,7 @@ def tile_myinterleavedmodule_t_kernel(tc, x, W_dense, W_sparse, grad_out, out):
             transpose_bank(0, b, grouped, nc.scalar.copy)
             quantise_tiles(b * BANK_TILES, BANK_TILES, grouped, codes, scales)
         quantise_weight("sparse")
+        idle_passes(GAP_PASSES)
         open_sums = []
         for j in range(HALF_TILES):
             sums = sum_banks.tile([P, COLS], F32, name="sums")

@@ -23,6 +23,8 @@ HALF_TILES = ROUND_TILES // 2
 ROUNDS = TOKEN_TILES // ROUND_TILES
 BANK_TILES = 2
 ROUND_BANKS = ROUND_TILES // BANK_TILES
+GROUP_TILES = 2 * ROUND_TILES
+COARSE_ROUNDS = 4
 TILES_BEFORE_RUN = 2
 TILES_BEFORE_FIRST_RUN = 6
 WARM_UP_PASSES = 7
@@ -36,8 +38,8 @@ BYTES = TOKENS * K * 2 + 2 * K * COLS * 2 + TOKENS * COLS * 4
 def tile_myinterleavedmodule_t_kernel(tc, x, W_dense, W_sparse, grad_out, out):
     nc = tc.nc
 
-    grad_rows = grad_out.rearrange("(r p j) k -> r p (j k)", p=P, j=ROUND_TILES)
-    out_rows = out.rearrange("(r p j) c -> r p (j c)", p=P, j=ROUND_TILES)
+    grad_rows = grad_out.rearrange("(g p i) k -> g p (i k)", p=P, i=GROUP_TILES)
+    out_rows = out.rearrange("(g p i) c -> g p (i c)", p=P, i=GROUP_TILES)
 
     with ExitStack() as ctx:
         ctx.enter_context(tc.manual_schedule())
@@ -49,7 +51,8 @@ def tile_myinterleavedmodule_t_kernel(tc, x, W_dense, W_sparse, grad_out, out):
 
         weight_raw = {}
         grad_raw = [
-            keep.tile([P, ROUND_TILES * K], BF16, name="grad_raw%d" % r) for r in range(ROUNDS)
+            keep.tile([P, GROUP_TILES * K], BF16, name="grad_raw%d" % g)
+            for g in range(TOKEN_TILES // GROUP_TILES)
         ]
 
         def load_weight(name, weight):
@@ -60,10 +63,10 @@ def tile_myinterleavedmodule_t_kernel(tc, x, W_dense, W_sparse, grad_out, out):
             )
             weight_raw[name] = raw
 
-        def load_grad(r, first, count):
+        def load_grad(g, first, count):
             nc.sync.dma_start(
-                out=grad_raw[r][:, first * K : (first + count) * K],
-                in_=grad_rows[r, :, first * K : (first + count) * K],
+                out=grad_raw[g][:, first * K : (first + count) * K],
+                in_=grad_rows[g, :, first * K : (first + count) * K],
             )
 
         load_weight("dense", W_dense)
@@ -71,8 +74,9 @@ def tile_myinterleavedmodule_t_kernel(tc, x, W_dense, W_sparse, grad_out, out):
         load_grad(0, BANK_TILES, BANK_TILES)
         load_weight("sparse", W_sparse)
         load_grad(0, HALF_TILES, HALF_TILES)
-        for r in range(1, ROUNDS):
-            load_grad(r, 0, ROUND_TILES)
+        load_grad(0, ROUND_TILES, ROUND_TILES)
+        for g in range(1, TOKEN_TILES // GROUP_TILES):
+            load_grad(g, 0, GROUP_TILES)
 
         identity = keep.tile([P, P], F32, name="identity")
         make_identity(nc, identity[:])
@@ -112,10 +116,10 @@ def tile_myinterleavedmodule_t_kernel(tc, x, W_dense, W_sparse, grad_out, out):
             return grouped, codes, scales
 
         def transpose_bank(r, b, grouped, copy_out):
-            pairs = grad_raw[r][:].bitcast(F32)
+            pairs = grad_raw[r // 2][:].bitcast(F32)
             flipped = flipped_banks.tile([P, BANK_TILES * PAIRS], F32, name="flipped")
             for block in range(BANK_TILES * 2):
-                first = (b * BANK_TILES * 2 + block) * P
+                first = ((r % 2) * ROUND_TILES * 2 + b * BANK_TILES * 2 + block) * P
                 nc.tensor.transpose(
                     flipped[:, block * P : (block + 1) * P],
                     pairs[:, first : first + P],
@@ -157,8 +161,9 @@ def tile_myinterleavedmodule_t_kernel(tc, x, W_dense, W_sparse, grad_out, out):
             )
 
         def store(r, result, first, count):
+            in_group = (r % 2) * ROUND_TILES + first
             nc.sync.dma_start(
-                out=out_rows[r, :, first * COLS : (first + count) * COLS],
+                out=out_rows[r // 2, :, in_group * COLS : (in_group + count) * COLS],
                 in_=result[:, first * COLS : (first + count) * COLS],
             )
 
@@ -166,6 +171,9 @@ def tile_myinterleavedmodule_t_kernel(tc, x, W_dense, W_sparse, grad_out, out):
             nc.scalar.copy(out=result[:, j * COLS : (j + 1) * COLS], in_=sums[:])
             if r == ROUNDS - 1 and j >= HALF_TILES:
                 store(r, result, j, 1)
+            elif r < COARSE_ROUNDS:
+                if j + 1 == ROUND_TILES:
+                    store(r, result, 0, ROUND_TILES)
             elif (j + 1) % HALF_TILES == 0:
                 store(r, result, j + 1 - HALF_TILES, HALF_TILES)
 

@@ -25,6 +25,8 @@ BANK_TILES = 2
 ROUND_BANKS = ROUND_TILES // BANK_TILES
 GROUP_TILES = 2 * ROUND_TILES
 COARSE_ROUNDS = 4
+PAIRS_FROM = 16
+SINGLES_FROM = 4
 TILES_BEFORE_RUN = 2
 TILES_BEFORE_FIRST_RUN = 6
 WARM_UP_PASSES = 7
@@ -169,13 +171,17 @@ def tile_myinterleavedmodule_t_kernel(tc, x, W_dense, W_sparse, grad_out, out):
 
         def leave(r, j, sums, result):
             nc.scalar.copy(out=result[:, j * COLS : (j + 1) * COLS], in_=sums[:])
-            if r == ROUNDS - 1 and j >= HALF_TILES:
-                store(r, result, j, 1)
-            elif r < COARSE_ROUNDS:
-                if j + 1 == ROUND_TILES:
-                    store(r, result, 0, ROUND_TILES)
-            elif (j + 1) % HALF_TILES == 0:
-                store(r, result, j + 1 - HALF_TILES, HALF_TILES)
+            tiles_to_come = (ROUNDS - r) * ROUND_TILES - j
+            if r < COARSE_ROUNDS:
+                stored = ROUND_TILES
+            elif tiles_to_come > PAIRS_FROM:
+                stored = HALF_TILES
+            elif tiles_to_come > SINGLES_FROM:
+                stored = 2
+            else:
+                stored = 1
+            if (j + 1) % stored == 0:
+                store(r, result, j + 1 - stored, stored)
 
         def multiply(r, tiles, codes, scales, result):
             for j in tiles:

@@ -28,7 +28,7 @@ COARSE_ROUNDS = 4
 PAIRS_FROM = 16
 SINGLES_FROM = 4
 TILES_BEFORE_RUN = 2
-TILES_BEFORE_FIRST_RUN = 6
+TILES_BEFORE_FIRST_RUN = 4
 WARM_UP_PASSES = 7
 GAP_PASSES = 2
 VECTOR_COLS = 352
@@ -170,7 +170,9 @@ def tile_myinterleavedmodule_t_kernel(tc, x, W_dense, W_sparse, grad_out, out):
             )
 
         def leave(r, j, sums, result):
-            nc.scalar.copy(out=result[:, j * COLS : (j + 1) * COLS], in_=sums[:])
+            by_vector = r == ROUNDS - 1 and j % 2 == 1
+            copy_out = nc.vector.tensor_copy if by_vector else nc.scalar.copy
+            copy_out(out=result[:, j * COLS : (j + 1) * COLS], in_=sums[:])
             tiles_to_come = (ROUNDS - r) * ROUND_TILES - j
             if r < COARSE_ROUNDS:
                 stored = ROUND_TILES

@@ -98,9 +98,15 @@ def tile_myinterleavedmodule_t_kernel(tc, x, W_dense, W_sparse, grad_out, out):
 
         def quantise_weight(name):
             grouped = keep.tile([P, COLS, PACK], BF16, name="grouped_" + name, align_bytes=64)
-            by_column = weight_raw[name][:].rearrange("q t c -> q c t")
-            nc.vector.tensor_copy(out=grouped[:, :VECTOR_COLS, :], in_=by_column[:, :VECTOR_COLS, :])
-            nc.scalar.copy(out=grouped[:, VECTOR_COLS:, :], in_=by_column[:, VECTOR_COLS:, :])
+            raw = weight_raw[name]
+            nc.vector.tensor_copy(
+                out=grouped[:, :VECTOR_COLS, :].rearrange("q (c i) t -> q c t i", i=4),
+                in_=raw[:, :, :VECTOR_COLS].rearrange("q t (c i) -> q c t i", i=4),
+            )
+            nc.scalar.copy(
+                out=grouped[:, VECTOR_COLS:, :].rearrange("q (c i) t -> q c t i", i=4),
+                in_=raw[:, :, VECTOR_COLS:].rearrange("q t (c i) -> q c t i", i=4),
+            )
             codes = keep.tile([P, COLS], U32, name="codes_" + name, align_bytes=64)
             scales = keep.tile([P, COLS], U8, name="scales_" + name, align_bytes=64)
             nc.vector.quantize_mx(

@@ -18,13 +18,23 @@ COLS = 512
 PAIRS = K // 2
 
 TOKEN_TILES = TOKENS // P
+GROUP_TILES = 16
+GROUPS = TOKEN_TILES // GROUP_TILES
 ROUND_TILES = 8
-HALF_TILES = ROUND_TILES // 2
 ROUNDS = TOKEN_TILES // ROUND_TILES
+HALF_TILES = ROUND_TILES // 2
 BANK_TILES = 2
-ROUND_BANKS = ROUND_TILES // BANK_TILES
-GROUP_TILES = 2 * ROUND_TILES
-COARSE_ROUNDS = 4
+PSUM_BANKS = 8
+STAGES = [
+    (0, 0, ROUND_TILES),
+    (0, ROUND_TILES, ROUND_TILES),
+    (1, 0, GROUP_TILES),
+    (2, 0, GROUP_TILES),
+    (3, 0, ROUND_TILES),
+    (3, ROUND_TILES, ROUND_TILES),
+]
+EMPTY_FIRST = 6
+COARSE_ROUNDS = 2
 PAIRS_FROM = 16
 SINGLES_FROM = 4
 TILES_BEFORE_RUN = 2
@@ -48,14 +58,10 @@ def tile_myinterleavedmodule_t_kernel(tc, x, W_dense, W_sparse, grad_out, out):
         keep = ctx.enter_context(tc.tile_pool(name="keep", bufs=1))
         work = ctx.enter_context(tc.tile_pool(name="work", bufs=2))
         results = ctx.enter_context(tc.tile_pool(name="results", bufs=4))
-        flipped_banks = ctx.enter_context(tc.psum_pool(name="flipped_banks", bufs=ROUND_BANKS))
-        sum_banks = ctx.enter_context(tc.psum_pool(name="sum_banks", bufs=4))
+        banks = ctx.enter_context(tc.psum_pool(name="banks", bufs=PSUM_BANKS))
 
         weight_raw = {}
-        grad_raw = [
-            keep.tile([P, GROUP_TILES * K], BF16, name="grad_raw%d" % g)
-            for g in range(TOKEN_TILES // GROUP_TILES)
-        ]
+        grad_raw = [keep.tile([P, GROUP_TILES * K], BF16, name="grad_raw%d" % g) for g in range(GROUPS)]
 
         def load_weight(name, weight):
             raw = keep.tile([P, PACK, COLS], BF16, name="raw_" + name)
@@ -77,7 +83,7 @@ def tile_myinterleavedmodule_t_kernel(tc, x, W_dense, W_sparse, grad_out, out):
         load_weight("sparse", W_sparse)
         load_grad(0, HALF_TILES, HALF_TILES)
         load_grad(0, ROUND_TILES, ROUND_TILES)
-        for g in range(1, TOKEN_TILES // GROUP_TILES):
+        for g in range(1, GROUPS):
             load_grad(g, 0, GROUP_TILES)
 
         identity = keep.tile([P, P], F32, name="identity")
@@ -85,7 +91,7 @@ def tile_myinterleavedmodule_t_kernel(tc, x, W_dense, W_sparse, grad_out, out):
 
         zeros = keep.tile([P, COLS], BF16, name="zeros")
         nc.vector.memset(zeros[:], 0.0)
-        unread = sum_banks.tile([P, COLS], F32, name="sums")
+        unread = banks.tile([P, COLS], F32, name="bank")
 
         def idle_passes(count):
             for i in range(count):
@@ -117,17 +123,18 @@ def tile_myinterleavedmodule_t_kernel(tc, x, W_dense, W_sparse, grad_out, out):
             weight_codes[name] = codes
             weight_scales[name] = scales
 
-        def new_round():
-            grouped = work.tile([P, ROUND_TILES * K], BF16, name="grouped", align_bytes=64)
-            codes = work.tile([P, ROUND_TILES * P], U32, name="codes", align_bytes=64)
-            scales = work.tile([P, ROUND_TILES * P], U8, name="scales", align_bytes=64)
+        def new_stage():
+            grouped = work.tile([P, GROUP_TILES * K], BF16, name="grouped", align_bytes=64)
+            codes = work.tile([P, GROUP_TILES * P], U32, name="codes", align_bytes=64)
+            scales = work.tile([P, GROUP_TILES * P], U8, name="scales", align_bytes=64)
             return grouped, codes, scales
 
-        def transpose_bank(r, b, grouped, copy_out):
-            pairs = grad_raw[r // 2][:].bitcast(F32)
-            flipped = flipped_banks.tile([P, BANK_TILES * PAIRS], F32, name="flipped")
+        def transpose_bank(stage, b, grouped, copy_out):
+            g, first_tile, count = stage
+            pairs = grad_raw[g][:].bitcast(F32)
+            flipped = banks.tile([P, BANK_TILES * PAIRS], F32, name="bank")
             for block in range(BANK_TILES * 2):
-                first = ((r % 2) * ROUND_TILES * 2 + b * BANK_TILES * 2 + block) * P
+                first = ((first_tile + b * BANK_TILES) * 2 + block) * P
                 nc.tensor.transpose(
                     flipped[:, block * P : (block + 1) * P],
                     pairs[:, first : first + P],
@@ -148,12 +155,19 @@ def tile_myinterleavedmodule_t_kernel(tc, x, W_dense, W_sparse, grad_out, out):
                 in_=grouped[:, first * K : (first + count) * K],
             )
 
-        def transpose_and_quantise(r):
-            grouped, codes, scales = new_round()
-            for b in range(ROUND_BANKS):
-                transpose_bank(r, b, grouped, nc.vector.tensor_copy)
-                if (b + 1) * BANK_TILES % HALF_TILES == 0:
-                    quantise_tiles((b + 1) * BANK_TILES - HALF_TILES, HALF_TILES, grouped, codes, scales)
+        def transpose_and_quantise(stage):
+            grouped, codes, scales = new_stage()
+            run_banks = stage[2] // BANK_TILES
+            ahead = EMPTY_FIRST - 2 if run_banks > 4 else 0
+            quantised_tiles = 0
+            for b in range(run_banks):
+                transpose_bank(stage, b, grouped, nc.vector.tensor_copy)
+                emptied_tiles = (b + 1) * BANK_TILES
+                if b + 1 < run_banks:
+                    emptied_tiles -= ahead * BANK_TILES
+                while quantised_tiles + HALF_TILES <= emptied_tiles:
+                    quantise_tiles(quantised_tiles, HALF_TILES, grouped, codes, scales)
+                    quantised_tiles += HALF_TILES
             return codes, scales
 
         def product(name, j, codes, scales, sums):
@@ -168,18 +182,20 @@ def tile_myinterleavedmodule_t_kernel(tc, x, W_dense, W_sparse, grad_out, out):
                 stop=(name == "sparse"),
             )
 
-        def store(r, result, first, count):
-            in_group = (r % 2) * ROUND_TILES + first
-            nc.sync.dma_start(
-                out=out_rows[r // 2, :, in_group * COLS : (in_group + count) * COLS],
-                in_=result[:, first * COLS : (first + count) * COLS],
-            )
+        result_of_round = {}
 
-        def leave(r, j, sums, result):
-            by_vector = r == ROUNDS - 1 and j % 2 == 1
+        def leave(stage, j, sums):
+            g, first_tile, count = stage
+            in_group = first_tile + j
+            r = (g * GROUP_TILES + in_group) // ROUND_TILES
+            in_round = in_group % ROUND_TILES
+            if in_round == 0:
+                result_of_round[r] = results.tile([P, ROUND_TILES * COLS], F32, name="result")
+            result = result_of_round[r]
+            by_vector = r == ROUNDS - 1 and in_round % 2 == 1
             copy_out = nc.vector.tensor_copy if by_vector else nc.scalar.copy
-            copy_out(out=result[:, j * COLS : (j + 1) * COLS], in_=sums[:])
-            tiles_to_come = (ROUNDS - r) * ROUND_TILES - j
+            copy_out(out=result[:, in_round * COLS : (in_round + 1) * COLS], in_=sums[:])
+            tiles_to_come = (ROUNDS - r) * ROUND_TILES - in_round
             if r < COARSE_ROUNDS:
                 stored = ROUND_TILES
             elif tiles_to_come > PAIRS_FROM:
@@ -188,44 +204,46 @@ def tile_myinterleavedmodule_t_kernel(tc, x, W_dense, W_sparse, grad_out, out):
                 stored = 2
             else:
                 stored = 1
-            if (j + 1) % stored == 0:
-                store(r, result, j + 1 - stored, stored)
+            if (in_round + 1) % stored == 0:
+                nc.sync.dma_start(
+                    out=out_rows[g, :, (in_group + 1 - stored) * COLS : (in_group + 1) * COLS],
+                    in_=result[:, (in_round + 1 - stored) * COLS : (in_round + 1) * COLS],
+                )
 
-        def multiply(r, tiles, codes, scales, result):
+        def multiply(stage, tiles, codes, scales):
             for j in tiles:
-                sums = sum_banks.tile([P, COLS], F32, name="sums")
+                sums = banks.tile([P, COLS], F32, name="bank")
                 product("dense", j, codes, scales, sums)
                 product("sparse", j, codes, scales, sums)
-                leave(r, j, sums, result)
+                leave(stage, j, sums)
 
-        grouped, codes, scales = new_round()
-        result = results.tile([P, ROUND_TILES * COLS], F32, name="result")
+        head = STAGES[0]
+        grouped, codes, scales = new_stage()
         quantise_weight("dense")
         for b in range(HALF_TILES // BANK_TILES):
-            transpose_bank(0, b, grouped, nc.scalar.copy)
+            transpose_bank(head, b, grouped, nc.scalar.copy)
             quantise_tiles(b * BANK_TILES, BANK_TILES, grouped, codes, scales)
         quantise_weight("sparse")
         idle_passes(GAP_PASSES)
         open_sums = []
         for j in range(HALF_TILES):
-            sums = sum_banks.tile([P, COLS], F32, name="sums")
+            sums = banks.tile([P, COLS], F32, name="bank")
             product("dense", j, codes, scales, sums)
             open_sums.append(sums)
-        transpose_bank(0, 2, grouped, nc.scalar.copy)
-        transpose_bank(0, 3, grouped, nc.vector.tensor_copy)
+        transpose_bank(head, 2, grouped, nc.scalar.copy)
+        transpose_bank(head, 3, grouped, nc.vector.tensor_copy)
         quantise_tiles(2 * BANK_TILES, BANK_TILES, grouped, codes, scales)
         quantise_tiles(3 * BANK_TILES, BANK_TILES, grouped, codes, scales)
         for j in range(HALF_TILES):
             product("sparse", j, codes, scales, open_sums[j])
-            leave(0, j, open_sums[j], result)
-        multiply(0, range(HALF_TILES, TILES_BEFORE_FIRST_RUN), codes, scales, result)
-        quantised = transpose_and_quantise(1)
-        multiply(0, range(TILES_BEFORE_FIRST_RUN, ROUND_TILES), codes, scales, result)
+            leave(head, j, open_sums[j])
+        multiply(head, range(HALF_TILES, TILES_BEFORE_FIRST_RUN), codes, scales)
+        quantised = transpose_and_quantise(STAGES[1])
+        multiply(head, range(TILES_BEFORE_FIRST_RUN, ROUND_TILES), codes, scales)
 
-        for r in range(1, ROUNDS):
+        for s in range(1, len(STAGES)):
             codes, scales = quantised
-            result = results.tile([P, ROUND_TILES * COLS], F32, name="result")
-            multiply(r, range(TILES_BEFORE_RUN), codes, scales, result)
-            if r + 1 < ROUNDS:
-                quantised = transpose_and_quantise(r + 1)
-            multiply(r, range(TILES_BEFORE_RUN, ROUND_TILES), codes, scales, result)
+            multiply(STAGES[s], range(TILES_BEFORE_RUN), codes, scales)
+            if s + 1 < len(STAGES):
+                quantised = transpose_and_quantise(STAGES[s + 1])
+            multiply(STAGES[s], range(TILES_BEFORE_RUN, STAGES[s][2]), codes, scales)

@@ -192,8 +192,19 @@ def tile_myinterleavedmodule_t_kernel(tc, x, W_dense, W_sparse, grad_out, out):
             if in_round == 0:
                 result_of_round[r] = results.tile([P, ROUND_TILES * COLS], F32, name="result")
             result = result_of_round[r]
+            tiles_left = (ROUNDS - r) * ROUND_TILES - in_round
             by_vector = r == ROUNDS - 1 and in_round % 2 == 1
             copy_out = nc.vector.tensor_copy if by_vector else nc.scalar.copy
+            if tiles_left == 1:
+                for half in range(2):
+                    cols = slice(half * COLS // 2, (half + 1) * COLS // 2)
+                    at = in_round * COLS + half * COLS // 2
+                    copy_out(out=result[:, at : at + COLS // 2], in_=sums[:, cols])
+                    nc.sync.dma_start(
+                        out=out_rows[g, :, in_group * COLS + half * COLS // 2 : in_group * COLS + (half + 1) * COLS // 2],
+                        in_=result[:, at : at + COLS // 2],
+                    )
+                return
             copy_out(out=result[:, in_round * COLS : (in_round + 1) * COLS], in_=sums[:])
             tiles_to_come = (ROUNDS - r) * ROUND_TILES - in_round
             if r < COARSE_ROUNDS:

from contextlib import ExitStack

import concourse.mybir as mybir
from concourse.masks import make_identity

BF16 = mybir.dt.bfloat16
F32 = mybir.dt.float32
U32 = mybir.dt.uint32
U8 = mybir.dt.uint8
E4M3_X4 = mybir.dt.float8_e4m3fn_x4
E5M2_X4 = mybir.dt.float8_e5m2_x4

P = 128
PACK = 4
TOKENS = 8192
K = 512
COLS = 512
PAIRS = K // 2

TOKEN_TILES = TOKENS // P
GROUP_TILES = 16
GROUPS = TOKEN_TILES // GROUP_TILES
ROUND_TILES = 8
ROUNDS = TOKEN_TILES // ROUND_TILES
HALF_TILES = ROUND_TILES // 2
BANK_TILES = 2
PSUM_BANKS = 8
STAGES = [
    (0, 0, ROUND_TILES),
    (0, ROUND_TILES, ROUND_TILES),
    (1, 0, GROUP_TILES),
    (2, 0, GROUP_TILES),
    (3, 0, ROUND_TILES),
    (3, ROUND_TILES, ROUND_TILES),
]
EMPTY_FIRST = 6
COARSE_ROUNDS = 2
PAIRS_FROM = 16
SINGLES_FROM = 4
TILES_BEFORE_RUN = 2
TILES_BEFORE_FIRST_RUN = 4
WARM_UP_PASSES = 7
GAP_PASSES = 2
VECTOR_COLS = 352

FLOPS = 2 * 2 * TOKENS * K * COLS
BYTES = TOKENS * K * 2 + 2 * K * COLS * 2 + TOKENS * COLS * 4


def tile_myinterleavedmodule_t_kernel(tc, x, W_dense, W_sparse, grad_out, out):
    nc = tc.nc

    grad_rows = grad_out.rearrange("(g p i) k -> g p (i k)", p=P, i=GROUP_TILES)
    out_rows = out.rearrange("(g p i) c -> g p (i c)", p=P, i=GROUP_TILES)

    with ExitStack() as ctx:
        ctx.enter_context(tc.manual_schedule())
        keep = ctx.enter_context(tc.tile_pool(name="keep", bufs=1))
        work = ctx.enter_context(tc.tile_pool(name="work", bufs=2))
        results = ctx.enter_context(tc.tile_pool(name="results", bufs=4))
        banks = ctx.enter_context(tc.psum_pool(name="banks", bufs=PSUM_BANKS))

        weight_raw = {}
        grad_raw = [keep.tile([P, GROUP_TILES * K], BF16, name="grad_raw%d" % g) for g in range(GROUPS)]

        def load_weight(name, weight):
            raw = keep.tile([P, PACK, COLS], BF16, name="raw_" + name)
            nc.sync.dma_start(
                out=raw[:].rearrange("q (u e) c -> q u (e c)", u=2),
                in_=weight.rearrange("(u q e) c -> q u (e c)", u=2, e=2),
            )
            weight_raw[name] = raw

        def load_grad(g, first, count):
            nc.sync.dma_start(
                out=grad_raw[g][:, first * K : (first + count) * K],
                in_=grad_rows[g, :, first * K : (first + count) * K],
            )

        load_weight("dense", W_dense)
        load_grad(0, 0, BANK_TILES)
        load_grad(0, BANK_TILES, BANK_TILES)
        load_weight("sparse", W_sparse)
        load_grad(0, HALF_TILES, HALF_TILES)
        load_grad(0, ROUND_TILES, ROUND_TILES)
        for g in range(1, GROUPS):
            load_grad(g, 0, GROUP_TILES)

        identity = keep.tile([P, P], F32, name="identity")
        make_identity(nc, identity[:])

        zeros = keep.tile([P, COLS], BF16, name="zeros")
        nc.vector.memset(zeros[:], 0.0)
        unread = banks.tile([P, COLS], F32, name="bank")

        def idle_passes(count):
            for i in range(count):
                nc.tensor.matmul(unread[:], lhsT=zeros[:, :P], rhs=zeros[:], start=True, stop=True)

        idle_passes(WARM_UP_PASSES)

        weight_codes = {}
        weight_scales = {}

        def quantise_weight(name):
            grouped = keep.tile([P, COLS, PACK], BF16, name="grouped_" + name, align_bytes=64)
            raw = weight_raw[name]
            nc.vector.tensor_copy(
                out=grouped[:, :VECTOR_COLS, :].rearrange("q (c i) t -> q c t i", i=4),
                in_=raw[:, :, :VECTOR_COLS].rearrange("q t (c i) -> q c t i", i=4),
            )
            nc.scalar.copy(
                out=grouped[:, VECTOR_COLS:, :].rearrange("q (c i) t -> q c t i", i=4),
                in_=raw[:, :, VECTOR_COLS:].rearrange("q t (c i) -> q c t i", i=4),
            )
            codes = keep.tile([P, COLS], U32, name="codes_" + name, align_bytes=64)
            scales = keep.tile([P, COLS], U8, name="scales_" + name, align_bytes=64)
            nc.vector.quantize_mx(
                out=codes[:].bitcast(E4M3_X4),
                scales=scales[:],
                in_=grouped[:].rearrange("q c t -> q (c t)"),
            )
            weight_codes[name] = codes
            weight_scales[name] = scales

        def new_stage():
            grouped = work.tile([P, GROUP_TILES * K], BF16, name="grouped", align_bytes=64)
            codes = work.tile([P, GROUP_TILES * P], U32, name="codes", align_bytes=64)
            scales = work.tile([P, GROUP_TILES * P], U8, name="scales", align_bytes=64)
            return grouped, codes, scales

        def transpose_bank(stage, b, grouped, copy_out):
            g, first_tile, count = stage
            pairs = grad_raw[g][:].bitcast(F32)
            flipped = banks.tile([P, BANK_TILES * PAIRS], F32, name="bank")
            for block in range(BANK_TILES * 2):
                first = ((first_tile + b * BANK_TILES) * 2 + block) * P
                nc.tensor.transpose(
                    flipped[:, block * P : (block + 1) * P],
                    pairs[:, first : first + P],
                    identity[:],
                )
            copy_out(
                out=grouped[:]
                .bitcast(F32)[:, b * BANK_TILES * PAIRS : (b + 1) * BANK_TILES * PAIRS]
                .rearrange("q (j m u) -> q j m u", j=BANK_TILES, u=2),
                in_=flipped[:].rearrange("q (j u m) -> q j m u", j=BANK_TILES, u=2),
            )

        def quantise_tiles(first, count, grouped, codes, scales):
            words = slice(first * P, (first + count) * P)
            nc.vector.quantize_mx(
                out=codes[:, words].bitcast(E5M2_X4),
                scales=scales[:, words],
                in_=grouped[:, first * K : (first + count) * K],
            )

        def transpose_and_quantise(stage):
            grouped, codes, scales = new_stage()
            run_banks = stage[2] // BANK_TILES
            ahead = EMPTY_FIRST - 2 if run_banks > 4 else 0
            quantised_tiles = 0
            for b in range(run_banks):
                transpose_bank(stage, b, grouped, nc.vector.tensor_copy)
                emptied_tiles = (b + 1) * BANK_TILES
                if b + 1 < run_banks:
                    emptied_tiles -= ahead * BANK_TILES
                while quantised_tiles + HALF_TILES <= emptied_tiles:
                    quantise_tiles(quantised_tiles, HALF_TILES, grouped, codes, scales)
                    quantised_tiles += HALF_TILES
            return codes, scales

        def product(name, j, codes, scales, sums):
            tokens = slice(j * P, (j + 1) * P)
            nc.tensor.matmul_mx(
                out=sums[:],
                lhsT=codes[:, tokens].bitcast(E5M2_X4),
                lhsT_scale=scales[:, tokens],
                rhs=weight_codes[name][:].bitcast(E4M3_X4),
                rhs_scale=weight_scales[name][:],
                start=(name == "dense"),
                stop=(name == "sparse"),
            )

        result_of_round = {}

        def leave(stage, j, sums):
            g, first_tile, count = stage
            in_group = first_tile + j
            r = (g * GROUP_TILES + in_group) // ROUND_TILES
            in_round = in_group % ROUND_TILES
            if in_round == 0:
                result_of_round[r] = results.tile([P, ROUND_TILES * COLS], F32, name="result")
            result = result_of_round[r]
            tiles_left = (ROUNDS - r) * ROUND_TILES - in_round
            by_vector = r == ROUNDS - 1 and in_round % 2 == 1
            copy_out = nc.vector.tensor_copy if by_vector else nc.scalar.copy
            if tiles_left == 1:
                for half in range(2):
                    cols = slice(half * COLS // 2, (half + 1) * COLS // 2)
                    at = in_round * COLS + half * COLS // 2
                    copy_out(out=result[:, at : at + COLS // 2], in_=sums[:, cols])
                    nc.sync.dma_start(
                        out=out_rows[g, :, in_group * COLS + half * COLS // 2 : in_group * COLS + (half + 1) * COLS // 2],
                        in_=result[:, at : at + COLS // 2],
                    )
                return
            copy_out(out=result[:, in_round * COLS : (in_round + 1) * COLS], in_=sums[:])
            tiles_to_come = (ROUNDS - r) * ROUND_TILES - in_round
            if r < COARSE_ROUNDS:
                stored = ROUND_TILES
            elif tiles_to_come > PAIRS_FROM:
                stored = HALF_TILES
            elif tiles_to_come > SINGLES_FROM:
                stored = 2
            else:
                stored = 1
            if (in_round + 1) % stored == 0:
                nc.sync.dma_start(
                    out=out_rows[g, :, (in_group + 1 - stored) * COLS : (in_group + 1) * COLS],
                    in_=result[:, (in_round + 1 - stored) * COLS : (in_round + 1) * COLS],
                )

        def multiply(stage, tiles, codes, scales):
            for j in tiles:
                sums = banks.tile([P, COLS], F32, name="bank")
                product("dense", j, codes, scales, sums)
                product("sparse", j, codes, scales, sums)
                leave(stage, j, sums)

        head = STAGES[0]
        grouped, codes, scales = new_stage()
        quantise_weight("dense")
        for b in range(HALF_TILES // BANK_TILES):
            transpose_bank(head, b, grouped, nc.scalar.copy)
            quantise_tiles(b * BANK_TILES, BANK_TILES, grouped, codes, scales)
        quantise_weight("sparse")
        idle_passes(GAP_PASSES)
        open_sums = []
        for j in range(HALF_TILES):
            sums = banks.tile([P, COLS], F32, name="bank")
            product("dense", j, codes, scales, sums)
            open_sums.append(sums)
        transpose_bank(head, 2, grouped, nc.scalar.copy)
        transpose_bank(head, 3, grouped, nc.vector.tensor_copy)
        quantise_tiles(2 * BANK_TILES, BANK_TILES, grouped, codes, scales)
        quantise_tiles(3 * BANK_TILES, BANK_TILES, grouped, codes, scales)
        for j in range(HALF_TILES):
            product("sparse", j, codes, scales, open_sums[j])
            leave(head, j, open_sums[j])
        multiply(head, range(HALF_TILES, TILES_BEFORE_FIRST_RUN), codes, scales)
        quantised = transpose_and_quantise(STAGES[1])
        multiply(head, range(TILES_BEFORE_FIRST_RUN, ROUND_TILES), codes, scales)

        for s in range(1, len(STAGES)):
            codes, scales = quantised
            multiply(STAGES[s], range(TILES_BEFORE_RUN), codes, scales)
            if s + 1 < len(STAGES):
                quantised = transpose_and_quantise(STAGES[s + 1])
            multiply(STAGES[s], range(TILES_BEFORE_RUN, STAGES[s][2]), codes, scales)
